import numpy as np
import ml_dtypes


def mxq(x, axis, fmt="e4m3"):
    dtype, down = {"e4m3": (ml_dtypes.float8_e4m3fn, 7), "e5m2": (ml_dtypes.float8_e5m2, 14)}[fmt]
    v = np.moveaxis(np.asarray(x, np.float32).astype(ml_dtypes.bfloat16).astype(np.float64), axis, -1)
    blocks = v.reshape(v.shape[:-1] + (-1, 32))
    amax = np.abs(blocks).max(-1, keepdims=True)
    byte = np.maximum(np.where(amax > 0, np.frexp(amax)[1] - 1 + 127, 0) - down, 1)
    scale = np.exp2(byte - 127.0)
    codes = (blocks / scale).astype(np.float32).astype(dtype).astype(np.float64)
    return np.moveaxis((codes * scale).reshape(v.shape), -1, axis)


WIDE = False


def mx_kscale(k):
    if not WIDE:
        return np.ones(k)
    levels = np.array([10, -10, 5, -5, 0])
    a = np.random.permutation(np.resize(levels, k // 512 * 4)).reshape(k // 512, 4)
    idx = np.arange(k)
    return np.exp2(a[idx // 512, idx % 128 // 32])


BF16 = ml_dtypes.bfloat16


def bf(x):
    return np.asarray(x, np.float32).astype(BF16)


def f64(x):
    return np.asarray(x).astype(np.float64)


B, S, E, H, HKV, D, F, M0, M1 = 2, 4096, 512, 1, 1, 128, 8192, 48, 40
M2 = D - M0 - M1
ROPE_BASE = 1000000.0
EPS = 1e-6


def rms_norm(v, w):
    return w * (v / np.sqrt(np.mean(v * v, axis=-1, keepdims=True) + EPS))


def mrope_cos_sin():
    t = np.arange(S, dtype=np.float64)
    parts = []
    for sd in (M0, M1, M2):
        inv_freq = 1.0 / ROPE_BASE ** (np.arange(0, sd, 2, dtype=np.float64) / sd)
        freqs = t[:, None] * inv_freq[None, :]
        parts.append(np.concatenate([freqs, freqs], -1))
    emb = np.concatenate(parts, -1)
    return np.cos(emb), np.sin(emb)


def rotate_half(v):
    d = D // 2
    return np.concatenate([-v[..., d:], v[..., :d]], -1)


def setup_inputs():
    s = mx_kscale(E)
    row = 0.5 + 1.5 * np.random.random_sample((B, S, 1))
    return {"x": bf(np.random.standard_normal((B, S, E)) * row),
            "ln1_w": bf((1.0 + 0.1 * np.random.standard_normal(E)) * s),
            "wq": bf(np.random.standard_normal((H * D, E)) / np.sqrt(E) / s),
            "wk": bf(np.random.standard_normal((HKV * D, E)) / np.sqrt(E) / s),
            "wv": bf(np.random.standard_normal((HKV * D, E)) / np.sqrt(E) / s),
            "q_norm_w": bf(1.0 + 0.1 * np.random.standard_normal(D)),
            "k_norm_w": bf(1.0 + 0.1 * np.random.standard_normal(D))}


def reference(x, ln1_w, wq, wk, wv, q_norm_w, k_norm_w):
    hq = mxq(rms_norm(f64(x), f64(ln1_w)), 2, "e4m3")
    q = (hq @ mxq(f64(wq), 1, "e4m3").T).reshape(B, S, H, D).transpose(0, 2, 1, 3)
    k = (hq @ mxq(f64(wk), 1, "e4m3").T).reshape(B, S, HKV, D).transpose(0, 2, 1, 3)
    v = (hq @ mxq(f64(wv), 1, "e4m3").T).reshape(B, S, HKV, D).transpose(0, 2, 1, 3)
    q = rms_norm(q, f64(q_norm_w))
    k = rms_norm(k, f64(k_norm_w))
    cos, sin = mrope_cos_sin()
    q = q * cos + rotate_half(q) * sin
    k = k * cos + rotate_half(k) * sin
    return q, k, v

@@ -1,0 +1,441 @@
+import math
+from contextlib import ExitStack
+
+import concourse.mybir as mybir
+from concourse.masks import make_identity
+
+F32 = mybir.dt.float32
+BF16 = mybir.dt.bfloat16
+I32 = mybir.dt.int32
+U32 = mybir.dt.uint32
+U8 = mybir.dt.uint8
+FP8X4 = mybir.dt.float8_e4m3fn_x4
+ACT = mybir.ActivationFunctionType
+ALU = mybir.AluOpType
+
+P = 128
+FLOPS = 2 * 8192 * 512 * 384
+ROPE_BASE = 1000000.0
+EPS = 1e-6
+NCH = 16
+PINNED = False
+GROUPS = ((0, 4), (4, 4), (8, 8), (16, 16))
+
+
+def turn_rates():
+    rates = []
+    for sd in (48, 40):
+        for j in range(sd // 2):
+            rates.append(1.0 / ROPE_BASE ** (2.0 * j / sd) / (2.0 * math.pi))
+    return rates
+
+
+def tile_selectivetransformerlayer_pa_t_kernel(
+    tc, x, ln1_w, wq, wk, wv, q_norm_w, k_norm_w, out_0, out_1, out_2
+):
+    nc = tc.nc
+    outs = (out_0, out_1, out_2)
+    with ExitStack() as ctx:
+        const = ctx.enter_context(tc.tile_pool(name="const", bufs=1))
+        xpool = ctx.enter_context(tc.tile_pool(name="xpool", bufs=5))
+        hpool = ctx.enter_context(tc.tile_pool(name="hpool", bufs=2))
+        gpool = ctx.enter_context(tc.tile_pool(name="gpool", bufs=2))
+        ppool = ctx.enter_context(tc.tile_pool(name="ppool", bufs=2))
+        opool = ctx.enter_context(tc.tile_pool(name="opool", bufs=3))
+        small = ctx.enter_context(tc.tile_pool(name="small", bufs=8))
+        junkp = ctx.enter_context(tc.tile_pool(name="junkp", bufs=4))
+        ps_w = ctx.enter_context(tc.psum_pool(name="ps_w", bufs=1))
+        ps_s = ctx.enter_context(tc.psum_pool(name="ps_s", bufs=1))
+        ps_t = ctx.enter_context(tc.psum_pool(name="ps_t", bufs=2))
+        ps_o = ctx.enter_context(tc.psum_pool(name="ps_o", bufs=4))
+
+        X = {}
+        SS = {}
+        RS = {}
+        H = {}
+        PT = {}
+        GQ = {}
+        CD = {}
+        PO = {}
+        RQ = {}
+        PR = {}
+        OQ = {}
+        OV = {}
+        TAB = {}
+
+        def load(n):
+            ch, b = n // 2, n % 2
+            xt = xpool.tile([P, 8, 256], BF16, name="xt")
+            for j2 in range(2):
+                nc.sync.dma_start(
+                    out=xt[j2:P:2, :, :],
+                    in_=x[b, 512 * ch : 512 * ch + 512, 256 * j2 : 256 * j2 + 256].rearrange(
+                        "(a g) c -> a g c", g=8
+                    ),
+                )
+            X[n] = xt
+
+        load(0)
+        load(1)
+
+        ones = const.tile([P, 1], F32, name="ones")
+        nc.vector.memset(ones[:], 1.0)
+        eps = const.tile([P, 1], F32, name="eps")
+        nc.vector.tensor_scalar(out=eps[:], in0=ones[:], scalar1=EPS, scalar2=None, op0=ALU.mult)
+        half_pi = const.tile([P, 1], F32, name="half_pi")
+        nc.vector.tensor_scalar(
+            out=half_pi[:], in0=ones[:], scalar1=math.pi / 2.0, scalar2=None, op0=ALU.mult
+        )
+        sel = const.tile([P, 64, 2], BF16, name="sel")
+        nc.vector.memset(sel[:], 0.0)
+        nc.vector.memset(sel[0:1, :, 0], 1.0)
+        nc.vector.memset(sel[32:33, :, 1], 1.0)
+        rows = const.tile([P, 512], BF16, name="rows")
+        nc.vector.memset(rows[:], 0.0)
+        for r, half in ((0, 0), (32, 1)):
+            nc.scalar.dma_start(
+                out=rows[r : r + 1, 0:256],
+                in_=ln1_w[256 * half : 256 * half + 256].rearrange("(o n) -> o n", o=1),
+            )
+        w_sb = const.tile([P, 3, 512], BF16, name="w_sb")
+        for wi, w in enumerate((wq, wk, wv)):
+            nc.scalar.dma_start(out=w_sb[:, wi, :], in_=w)
+        for r in (0, 32):
+            nc.scalar.dma_start(
+                out=rows[r : r + 1, 256:384], in_=q_norm_w.rearrange("(o n) -> o n", o=1)
+            )
+            nc.scalar.dma_start(
+                out=rows[r : r + 1, 384:512], in_=k_norm_w.rearrange("(o n) -> o n", o=1)
+            )
+
+        ident_f = const.tile([P, P], F32, name="ident_f")
+        make_identity(nc, ident_f[:])
+        pos_i = const.tile([P, 32], I32, name="pos_i")
+        nc.gpsimd.iota(pos_i[:], pattern=[[512, 8], [1, 4]], base=0, channel_multiplier=4)
+
+        rate = const.tile([P, 44], F32, name="rate")
+        for d, g in enumerate(turn_rates()):
+            nc.vector.tensor_scalar(
+                out=rate[:, d : d + 1], in0=ones[:], scalar1=g, scalar2=None, op0=ALU.mult
+            )
+        pos_f = const.tile([P, 32], F32, name="pos_f")
+        nc.vector.tensor_copy(out=pos_f[:], in_=pos_i[:])
+
+        ident_b = const.tile([P, P], BF16, name="ident_b")
+        nc.vector.tensor_copy(out=ident_b[:], in_=ident_f[:])
+        idv = ident_f[:].rearrange("p (a e) -> p a e", e=2)
+        pair_half = const.tile([P, 64], F32, name="pair_half")
+        nc.vector.tensor_tensor(out=pair_half[:], in0=idv[:, :, 0], in1=idv[:, :, 1], op=ALU.add)
+        pair_sum = const.tile([P, 64, 2], F32, name="pair_sum")
+        nc.vector.tensor_copy(
+            out=pair_sum[:], in_=pair_half[:].unsqueeze(2).to_broadcast([P, 64, 2])
+        )
+
+        spread = ps_w.tile([P, 512], F32, name="spread")
+        nc.tensor.matmul(
+            out=spread[:],
+            lhsT=sel[:].rearrange("p a e -> p (a e)"),
+            rhs=rows[:],
+            start=True,
+            stop=True,
+        )
+
+        turns = const.tile([P, 32, 44], F32, name="turns")
+        nc.vector.tensor_tensor(
+            out=turns[:],
+            in0=pos_f[:].unsqueeze(2).to_broadcast([P, 32, 44]),
+            in1=rate[:].unsqueeze(1).to_broadcast([P, 32, 44]),
+            op=ALU.mult,
+        )
+        whole_c = const.tile([P, 32, 44], I32, name="whole_c")
+        nc.vector.tensor_copy(out=whole_c[:], in_=turns[:])
+        trig_c = const.tile([P, 32, 44], F32, name="trig_c")
+        nc.vector.tensor_tensor(out=trig_c[:], in0=turns[:], in1=whole_c[:], op=ALU.subtract)
+        whole_s = const.tile([P, 32, 44], I32, name="whole_s")
+        nc.vector.tensor_scalar(
+            out=whole_s[:], in0=turns[:], scalar1=-0.25, scalar2=None, op0=ALU.add
+        )
+        trig_s = const.tile([P, 32, 44], F32, name="trig_s")
+        nc.vector.scalar_tensor_tensor(
+            out=trig_s[:],
+            in0=turns[:],
+            scalar=-0.25,
+            in1=whole_s[:],
+            op0=ALU.add,
+            op1=ALU.subtract,
+        )
+        for tr in (trig_c, trig_s):
+            nc.scalar.activation(out=tr[:], in_=tr[:], func=ACT.Abs)
+            nc.scalar.activation(
+                out=tr[:], in_=tr[:], func=ACT.Sin, scale=-2.0 * math.pi, bias=half_pi[:, 0:1]
+            )
+
+        gw = const.tile([P, 512, 4], BF16, name="gw", align_bytes=64)
+        for wi in range(3):
+            pw = ps_t.tile([P, 2, 512], BF16, name="pt")
+            for t in range(4):
+                blk = 2 * (t % 2) + t // 2
+                nc.tensor.transpose(
+                    out=pw[:, 0, 128 * t : 128 * t + 128],
+                    in_=w_sb[:, wi, 128 * blk : 128 * blk + 128],
+                    identity=ident_b[:],
+                )
+            src = pw[:, 0, :].rearrange("p (t n) -> p n t", t=4)
+            base = 192 * wi
+            nc.vector.tensor_copy(out=gw[:, base : base + 128, :], in_=src)
+            if wi < 2:
+                nc.vector.tensor_copy(out=gw[:, base + 128 : base + 192, :], in_=src[:, 0:64, :])
+        w_codes = const.tile([P, 512], U32, name="w_codes", align_bytes=64)
+        w_scales = const.tile([P, 512], U8, name="w_scales", align_bytes=64)
+        nc.vector.quantize_mx(
+            out=w_codes[:].bitcast(FP8X4),
+            scales=w_scales[:],
+            in_=gw[:].rearrange("p n t -> p (n t)"),
+        )
+
+        wn = spread[:, 256:512].rearrange("p (q h c) -> p q h c", q=2, h=2)
+        w_cos = const.tile([P, 2, 2, 64], F32, name="w_cos")
+        nc.vector.tensor_copy(out=w_cos[:], in_=wn)
+        w_sin = const.tile([P, 2, 2, 64], F32, name="w_sin")
+        nc.vector.tensor_scalar(
+            out=w_sin[:, :, 0, :], in0=wn[:, :, 1, :], scalar1=-1.0, scalar2=None, op0=ALU.mult
+        )
+        nc.vector.tensor_copy(out=w_sin[:, :, 1, :], in_=wn[:, :, 0, :])
+
+        def fold_ops(grp):
+            t0, nt = GROUPS[grp]
+            tab = const.tile([P, 2, nt, 2, 128], F32, name="tab%d" % grp)
+            TAB[grp] = tab
+            ops = []
+            for ab, (tr, wrow) in enumerate(((trig_c, w_cos), (trig_s, w_sin))):
+                wflat = wrow[:].rearrange("p q h c -> p q (h c)")
+                for qk in range(2):
+                    for c0, reps, d0, nd in ((0, 2, 0, 24), (48, 4, 24, 20)):
+                        ops.append((tab, ab, qk, c0, reps, d0, nd, tr, wflat, t0, nt))
+            return ops
+
+        def fold_one(op):
+            tab, ab, qk, c0, reps, d0, nd, tr, wflat, t0, nt = op
+            nc.gpsimd.tensor_tensor(
+                out=tab[:, ab, :, qk, c0 : c0 + reps * nd].rearrange("p t (r d) -> p t r d", r=reps),
+                in0=tr[:, t0 : t0 + nt, d0 : d0 + nd].unsqueeze(2).to_broadcast([P, nt, reps, nd]),
+                in1=wflat[:, qk, c0 : c0 + reps * nd]
+                .rearrange("p (r d) -> p r d", r=reps)
+                .unsqueeze(1)
+                .to_broadcast([P, nt, reps, nd]),
+                op=ALU.mult,
+            )
+
+        def table_of(tau):
+            for grp, (t0, nt) in enumerate(GROUPS):
+                if t0 <= tau < t0 + nt:
+                    return TAB[grp], tau - t0
+            return None, 0
+
+        def squares(n, i):
+            if i == 0:
+                ss = small.tile([P, 8], F32, name="ss")
+                SS[n] = ss
+            for g in (i, 4 + i):
+                junk = junkp.tile([P, 256], BF16, name="junk")
+                nc.scalar.activation(
+                    out=junk[:], in_=X[n][:, g, :], func=ACT.Square, accum_out=SS[n][:, g : g + 1]
+                )
+
+        def pairsum(n):
+            pss = ps_s.tile([P, 8], F32, name="pss")
+            nc.tensor.matmul(
+                out=pss[:],
+                lhsT=pair_sum[:].rearrange("p a e -> p (a e)"),
+                rhs=SS[n][:],
+                start=True,
+                stop=True,
+            )
+            SS[n] = pss
+
+        def rstd(n):
+            root = small.tile([P, 8], F32, name="root")
+            nc.scalar.activation(
+                out=root[:], in_=SS[n][:], func=ACT.Sqrt, scale=1.0 / 512.0, bias=eps[:, 0:1]
+            )
+            rs = small.tile([P, 8], F32, name="rs")
+            nc.vector.reciprocal(out=rs[:], in_=root[:])
+            RS[n] = rs
+
+        def normalise(n, i):
+            if i == 0:
+                ht = hpool.tile([P, 8, 256], BF16, name="ht")
+                H[n] = ht
+            for g in (i, 4 + i):
+                nc.vector.scalar_tensor_tensor(
+                    out=H[n][:, g, :],
+                    in0=X[n][:, g, :],
+                    scalar=RS[n][:, g : g + 1],
+                    in1=spread[:, 0:256],
+                    op0=ALU.mult,
+                    op1=ALU.mult,
+                )
+
+        def transposes(n, hf):
+            pt = ps_t.tile([P, 2, 512], BF16, name="pt")
+            PT[(n, hf)] = pt
+            for i2 in range(2):
+                i = 2 * hf + i2
+                view = pt[:, i2, :].rearrange("p (a r e) -> p a r e", r=4, e=2)
+                for hh in range(2):
+                    for u in range(2):
+                        nc.tensor.transpose(
+                            out=view[:, :, 2 * hh + u, :],
+                            in_=H[n][:, 4 * hh + i, 128 * u : 128 * u + 128],
+                            identity=ident_b[:],
+                        )
+
+        def evacuate(n, hf):
+            if hf == 0:
+                gq = gpool.tile([P, 2048], BF16, name="gq", align_bytes=64)
+                GQ[n] = gq
+            nc.scalar.copy(
+                out=GQ[n][:, 1024 * hf : 1024 * hf + 1024],
+                in_=PT[(n, hf)][:].rearrange("p i c -> p (i c)"),
+            )
+
+        def quantise(n, hf):
+            if hf == 0:
+                codes = gpool.tile([P, 512], U32, name="codes", align_bytes=64)
+                scl = gpool.tile([P, 512], U8, name="scl", align_bytes=64)
+                CD[n] = (codes, scl)
+            codes, scl = CD[n]
+            nc.vector.quantize_mx(
+                out=codes[:, 256 * hf : 256 * hf + 256].bitcast(FP8X4),
+                scales=scl[:, 256 * hf : 256 * hf + 256],
+                in_=GQ[n][:, 1024 * hf : 1024 * hf + 1024],
+            )
+
+        def project(n, i):
+            codes, scl = CD[n]
+            po = ps_o.tile([P, 512], F32, name="po")
+            PO[(n, i)] = po
+            nc.tensor.matmul_mx(
+                out=po[:],
+                lhsT=codes[:, 128 * i : 128 * i + 128].bitcast(FP8X4),
+                lhsT_scale=scl[:, 128 * i : 128 * i + 128],
+                rhs=w_codes[:].bitcast(FP8X4),
+                rhs_scale=w_scales[:],
+                start=True,
+                stop=True,
+            )
+
+        def head_stats(n, i):
+            po = PO[(n, i)]
+            if i == 0:
+                ov = opool.tile([P, 4, 128], F32, name="ov")
+                OV[n] = ov
+            sq = small.tile([P, 2], F32, name="sq")
+            for qk in range(2):
+                junk2 = junkp.tile([P, 128], BF16, name="junk2")
+                nc.scalar.activation(
+                    out=junk2[:],
+                    in_=po[:, 192 * qk : 192 * qk + 128],
+                    func=ACT.Square,
+                    accum_out=sq[:, qk : qk + 1],
+                )
+            nc.scalar.copy(out=OV[n][:, i, :], in_=po[:, 384:512])
+            root2 = small.tile([P, 2], F32, name="root2")
+            nc.scalar.activation(
+                out=root2[:], in_=sq[:], func=ACT.Sqrt, scale=1.0 / 128.0, bias=eps[:, 0:1]
+            )
+            rq = small.tile([P, 2], F32, name="rq")
+            nc.vector.reciprocal(out=rq[:], in_=root2[:])
+            RQ[(n, i)] = rq
+
+        def rope_products(n, i):
+            po = PO[(n, i)]
+            rq = RQ[(n, i)]
+            if i == 0:
+                pr = ppool.tile([P, 2, 4, 2, 128], F32, name="pr")
+                PR[n] = pr
+            tab, tl = table_of(4 * (n // 2) + i)
+            for qk in range(2):
+                for ab in range(2):
+                    nc.vector.scalar_tensor_tensor(
+                        out=PR[n][:, qk, i, ab, :],
+                        in0=po[:, 192 * qk + 64 * ab : 192 * qk + 64 * ab + 128],
+                        scalar=rq[:, qk : qk + 1],
+                        in1=tab[:, ab, tl, qk, :],
+                        op0=ALU.mult,
+                        op1=ALU.mult,
+                    )
+
+        def rope_add(n, hf):
+            if hf == 0:
+                oq = opool.tile([P, 2, 4, 128], F32, name="oq")
+                OQ[n] = oq
+            nc.gpsimd.tensor_tensor(
+                out=OQ[n][:, :, 2 * hf : 2 * hf + 2, :],
+                in0=PR[n][:, :, 2 * hf : 2 * hf + 2, 0, :],
+                in1=PR[n][:, :, 2 * hf : 2 * hf + 2, 1, :],
+                op=ALU.add,
+            )
+
+        def store(n):
+            ch, b = n // 2, n % 2
+            for k in range(3):
+                src_t = OQ[n][:, k, :, :] if k < 2 else OV[n][:]
+                nc.sync.dma_start(
+                    out=outs[k][b, 0, 512 * ch : 512 * ch + 512, :].rearrange(
+                        "(m i) d -> m (i d)", i=4
+                    ),
+                    in_=src_t.rearrange("p i d -> p (i d)"),
+                )
+
+        pending = []
+        cursor = [0]
+        for grp in range(2):
+            for op in fold_ops(grp):
+                fold_one(op)
+        for grp in range(2, 4):
+            pending.extend(fold_ops(grp))
+
+        def ok(n):
+            return 0 <= n < NCH
+
+        def body():
+            for k in range(-3, NCH):
+                if ok(k + 4) and k + 4 >= 2:
+                    load(k + 4)
+                if ok(k + 2):
+                    rstd(k + 2)
+                for hf in range(2):
+                    if ok(k + 1):
+                        evacuate(k + 1, hf)
+                        quantise(k + 1, hf)
+                    for i in (2 * hf, 2 * hf + 1):
+                        if ok(k):
+                            head_stats(k, i)
+                            rope_products(k, i)
+                        if ok(k + 3):
+                            squares(k + 3, i)
+                        if ok(k + 2):
+                            normalise(k + 2, i)
+                    if ok(k + 2):
+                        transposes(k + 2, hf)
+                    if ok(k + 1):
+                        project(k + 1, 2 * hf)
+                        project(k + 1, 2 * hf + 1)
+                    if ok(k):
+                        rope_add(k, hf)
+                    if k >= -1:
+                        for rep in range(2):
+                            if cursor[0] < len(pending):
+                                fold_one(pending[cursor[0]])
+                                cursor[0] = cursor[0] + 1
+                if ok(k + 3):
+                    pairsum(k + 3)
+                if ok(k):
+                    store(k)
+
+        if PINNED:
+            with tc.manual_schedule():
+                body()
+        else:
+            body()

@@ -18,8 +18,12 @@ FLOPS = 2 * 8192 * 512 * 384
 ROPE_BASE = 1000000.0
 EPS = 1e-6
 NCH = 16
-PINNED = False
-GROUPS = ((0, 4), (4, 4), (8, 8), (16, 16))
+PINNED = True
+GROUPS = ((0, 4), (4, 4), (8, 8), (16, 8), (24, 8))
+VECTOR_GROUPS = 2
+FOLDS_PER_ROUND = 2
+V_COPIES = ()
+ORDER8 = (0, 4, 1, 5, 2, 6, 3, 7)
 
 
 def turn_rates():
@@ -37,8 +41,8 @@ def tile_selectivetransformerlayer_pa_t_kernel(
     outs = (out_0, out_1, out_2)
     with ExitStack() as ctx:
         const = ctx.enter_context(tc.tile_pool(name="const", bufs=1))
-        xpool = ctx.enter_context(tc.tile_pool(name="xpool", bufs=5))
-        hpool = ctx.enter_context(tc.tile_pool(name="hpool", bufs=2))
+        xpool = ctx.enter_context(tc.tile_pool(name="xpool", bufs=6))
+        hpool = ctx.enter_context(tc.tile_pool(name="hpool", bufs=3))
         gpool = ctx.enter_context(tc.tile_pool(name="gpool", bufs=2))
         ppool = ctx.enter_context(tc.tile_pool(name="ppool", bufs=2))
         opool = ctx.enter_context(tc.tile_pool(name="opool", bufs=3))
@@ -49,14 +53,20 @@ def tile_selectivetransformerlayer_pa_t_kernel(
         ps_t = ctx.enter_context(tc.psum_pool(name="ps_t", bufs=2))
         ps_o = ctx.enter_context(tc.psum_pool(name="ps_o", bufs=4))
 
+        if PINNED:
+            ctx.enter_context(tc.manual_schedule())
+
         X = {}
         SS = {}
+        RT = {}
         RS = {}
         H = {}
         PT = {}
         GQ = {}
         CD = {}
         PO = {}
+        SQ = {}
+        R2 = {}
         RQ = {}
         PR = {}
         OQ = {}
@@ -75,17 +85,11 @@ def tile_selectivetransformerlayer_pa_t_kernel(
                 )
             X[n] = xt
 
-        load(0)
-        load(1)
+        for n in range(4):
+            load(n)
 
         ones = const.tile([P, 1], F32, name="ones")
         nc.vector.memset(ones[:], 1.0)
-        eps = const.tile([P, 1], F32, name="eps")
-        nc.vector.tensor_scalar(out=eps[:], in0=ones[:], scalar1=EPS, scalar2=None, op0=ALU.mult)
-        half_pi = const.tile([P, 1], F32, name="half_pi")
-        nc.vector.tensor_scalar(
-            out=half_pi[:], in0=ones[:], scalar1=math.pi / 2.0, scalar2=None, op0=ALU.mult
-        )
         sel = const.tile([P, 64, 2], BF16, name="sel")
         nc.vector.memset(sel[:], 0.0)
         nc.vector.memset(sel[0:1, :, 0], 1.0)
@@ -107,19 +111,13 @@ def tile_selectivetransformerlayer_pa_t_kernel(
             nc.scalar.dma_start(
                 out=rows[r : r + 1, 384:512], in_=k_norm_w.rearrange("(o n) -> o n", o=1)
             )
+        warm = const.tile([P, 1], F32, name="warm")
+        nc.scalar.activation(out=warm[:], in_=ones[:], func=ACT.Sin)
 
         ident_f = const.tile([P, P], F32, name="ident_f")
         make_identity(nc, ident_f[:])
         pos_i = const.tile([P, 32], I32, name="pos_i")
         nc.gpsimd.iota(pos_i[:], pattern=[[512, 8], [1, 4]], base=0, channel_multiplier=4)
-
-        rate = const.tile([P, 44], F32, name="rate")
-        for d, g in enumerate(turn_rates()):
-            nc.vector.tensor_scalar(
-                out=rate[:, d : d + 1], in0=ones[:], scalar1=g, scalar2=None, op0=ALU.mult
-            )
-        pos_f = const.tile([P, 32], F32, name="pos_f")
-        nc.vector.tensor_copy(out=pos_f[:], in_=pos_i[:])
 
         ident_b = const.tile([P, P], BF16, name="ident_b")
         nc.vector.tensor_copy(out=ident_b[:], in_=ident_f[:])
@@ -130,6 +128,19 @@ def tile_selectivetransformerlayer_pa_t_kernel(
         nc.vector.tensor_copy(
             out=pair_sum[:], in_=pair_half[:].unsqueeze(2).to_broadcast([P, 64, 2])
         )
+        eps = const.tile([P, 1], F32, name="eps")
+        nc.vector.tensor_scalar(out=eps[:], in0=ones[:], scalar1=EPS, scalar2=None, op0=ALU.mult)
+        half_pi = const.tile([P, 1], F32, name="half_pi")
+        nc.vector.tensor_scalar(
+            out=half_pi[:], in0=ones[:], scalar1=math.pi / 2.0, scalar2=None, op0=ALU.mult
+        )
+        rate = const.tile([P, 44], F32, name="rate")
+        for d, g in enumerate(turn_rates()):
+            nc.vector.tensor_scalar(
+                out=rate[:, d : d + 1], in0=ones[:], scalar1=g, scalar2=None, op0=ALU.mult
+            )
+        pos_f = const.tile([P, 32], F32, name="pos_f")
+        nc.vector.tensor_copy(out=pos_f[:], in_=pos_i[:])
 
         spread = ps_w.tile([P, 512], F32, name="spread")
         nc.tensor.matmul(
@@ -164,11 +175,6 @@ def tile_selectivetransformerlayer_pa_t_kernel(
             op0=ALU.add,
             op1=ALU.subtract,
         )
-        for tr in (trig_c, trig_s):
-            nc.scalar.activation(out=tr[:], in_=tr[:], func=ACT.Abs)
-            nc.scalar.activation(
-                out=tr[:], in_=tr[:], func=ACT.Sin, scale=-2.0 * math.pi, bias=half_pi[:, 0:1]
-            )
 
         gw = const.tile([P, 512, 4], BF16, name="gw", align_bytes=64)
         for wi in range(3):
@@ -214,9 +220,9 @@ def tile_selectivetransformerlayer_pa_t_kernel(
                         ops.append((tab, ab, qk, c0, reps, d0, nd, tr, wflat, t0, nt))
             return ops
 
-        def fold_one(op):
+        def fold_one(eng, op):
             tab, ab, qk, c0, reps, d0, nd, tr, wflat, t0, nt = op
-            nc.gpsimd.tensor_tensor(
+            eng.tensor_tensor(
                 out=tab[:, ab, :, qk, c0 : c0 + reps * nd].rearrange("p t (r d) -> p t r d", r=reps),
                 in0=tr[:, t0 : t0 + nt, d0 : d0 + nd].unsqueeze(2).to_broadcast([P, nt, reps, nd]),
                 in1=wflat[:, qk, c0 : c0 + reps * nd]
@@ -232,11 +238,11 @@ def tile_selectivetransformerlayer_pa_t_kernel(
                     return TAB[grp], tau - t0
             return None, 0
 
-        def squares(n, i):
-            if i == 0:
+        def squares(n, gs):
+            if n not in SS:
                 ss = small.tile([P, 8], F32, name="ss")
                 SS[n] = ss
-            for g in (i, 4 + i):
+            for g in gs:
                 junk = junkp.tile([P, 256], BF16, name="junk")
                 nc.scalar.activation(
                     out=junk[:], in_=X[n][:, g, :], func=ACT.Square, accum_out=SS[n][:, g : g + 1]
@@ -253,22 +259,24 @@ def tile_selectivetransformerlayer_pa_t_kernel(
             )
             SS[n] = pss
 
-        def rstd(n):
+        def rstd_root(n):
             root = small.tile([P, 8], F32, name="root")
             nc.scalar.activation(
                 out=root[:], in_=SS[n][:], func=ACT.Sqrt, scale=1.0 / 512.0, bias=eps[:, 0:1]
             )
+            RT[n] = root
+
+        def rstd_recip(n):
             rs = small.tile([P, 8], F32, name="rs")
-            nc.vector.reciprocal(out=rs[:], in_=root[:])
+            nc.vector.reciprocal(out=rs[:], in_=RT[n][:])
             RS[n] = rs
 
-        def normalise(n, i):
-            if i == 0:
-                ht = hpool.tile([P, 8, 256], BF16, name="ht")
-                H[n] = ht
-            for g in (i, 4 + i):
+        def normalise(n):
+            ht = hpool.tile([P, 8, 256], BF16, name="ht")
+            H[n] = ht
+            for g in ORDER8:
                 nc.vector.scalar_tensor_tensor(
-                    out=H[n][:, g, :],
+                    out=ht[:, g, :],
                     in0=X[n][:, g, :],
                     scalar=RS[n][:, g : g + 1],
                     in1=spread[:, 0:256],
@@ -299,17 +307,11 @@ def tile_selectivetransformerlayer_pa_t_kernel(
                 in_=PT[(n, hf)][:].rearrange("p i c -> p (i c)"),
             )
 
-        def quantise(n, hf):
-            if hf == 0:
-                codes = gpool.tile([P, 512], U32, name="codes", align_bytes=64)
-                scl = gpool.tile([P, 512], U8, name="scl", align_bytes=64)
-                CD[n] = (codes, scl)
-            codes, scl = CD[n]
-            nc.vector.quantize_mx(
-                out=codes[:, 256 * hf : 256 * hf + 256].bitcast(FP8X4),
-                scales=scl[:, 256 * hf : 256 * hf + 256],
-                in_=GQ[n][:, 1024 * hf : 1024 * hf + 1024],
-            )
+        def quantise(n):
+            codes = gpool.tile([P, 512], U32, name="codes", align_bytes=64)
+            scl = gpool.tile([P, 512], U8, name="scl", align_bytes=64)
+            CD[n] = (codes, scl)
+            nc.vector.quantize_mx(out=codes[:].bitcast(FP8X4), scales=scl[:], in_=GQ[n][:])
 
         def project(n, i):
             codes, scl = CD[n]
@@ -330,23 +332,37 @@ def tile_selectivetransformerlayer_pa_t_kernel(
             if i == 0:
                 ov = opool.tile([P, 4, 128], F32, name="ov")
                 OV[n] = ov
-            sq = small.tile([P, 2], F32, name="sq")
+                sq = small.tile([P, 4, 2], F32, name="sq")
+                SQ[n] = sq
             for qk in range(2):
                 junk2 = junkp.tile([P, 128], BF16, name="junk2")
                 nc.scalar.activation(
                     out=junk2[:],
                     in_=po[:, 192 * qk : 192 * qk + 128],
                     func=ACT.Square,
-                    accum_out=sq[:, qk : qk + 1],
+                    accum_out=SQ[n][:, i, qk : qk + 1],
                 )
-            nc.scalar.copy(out=OV[n][:, i, :], in_=po[:, 384:512])
-            root2 = small.tile([P, 2], F32, name="root2")
+            if i in V_COPIES:
+                nc.vector.tensor_copy(out=OV[n][:, i, :], in_=po[:, 384:512])
+            else:
+                nc.scalar.copy(out=OV[n][:, i, :], in_=po[:, 384:512])
+
+        def head_root(n, i0, ni):
+            root2 = small.tile([P, 4, 2], F32, name="root2")
             nc.scalar.activation(
-                out=root2[:], in_=sq[:], func=ACT.Sqrt, scale=1.0 / 128.0, bias=eps[:, 0:1]
+                out=root2[:, i0 : i0 + ni, :],
+                in_=SQ[n][:, i0 : i0 + ni, :],
+                func=ACT.Sqrt,
+                scale=1.0 / 128.0,
+                bias=eps[:, 0:1],
             )
-            rq = small.tile([P, 2], F32, name="rq")
-            nc.vector.reciprocal(out=rq[:], in_=root2[:])
-            RQ[(n, i)] = rq
+            R2[(n, i0)] = root2
+
+        def head_recip(n, i0, ni):
+            rq = small.tile([P, 4, 2], F32, name="rq")
+            nc.vector.reciprocal(out=rq[:, i0 : i0 + ni, :], in_=R2[(n, i0)][:, i0 : i0 + ni, :])
+            for i in range(i0, i0 + ni):
+                RQ[(n, i)] = rq
 
         def rope_products(n, i):
             po = PO[(n, i)]
@@ -360,26 +376,26 @@ def tile_selectivetransformerlayer_pa_t_kernel(
                     nc.vector.scalar_tensor_tensor(
                         out=PR[n][:, qk, i, ab, :],
                         in0=po[:, 192 * qk + 64 * ab : 192 * qk + 64 * ab + 128],
-                        scalar=rq[:, qk : qk + 1],
+                        scalar=rq[:, i, qk : qk + 1],
                         in1=tab[:, ab, tl, qk, :],
                         op0=ALU.mult,
                         op1=ALU.mult,
                     )
 
-        def rope_add(n, hf):
-            if hf == 0:
+        def rope_add(eng, n, i0, ni):
+            if i0 == 0:
                 oq = opool.tile([P, 2, 4, 128], F32, name="oq")
                 OQ[n] = oq
-            nc.gpsimd.tensor_tensor(
-                out=OQ[n][:, :, 2 * hf : 2 * hf + 2, :],
-                in0=PR[n][:, :, 2 * hf : 2 * hf + 2, 0, :],
-                in1=PR[n][:, :, 2 * hf : 2 * hf + 2, 1, :],
+            eng.tensor_tensor(
+                out=OQ[n][:, :, i0 : i0 + ni, :],
+                in0=PR[n][:, :, i0 : i0 + ni, 0, :],
+                in1=PR[n][:, :, i0 : i0 + ni, 1, :],
                 op=ALU.add,
             )
 
         def store(n):
             ch, b = n // 2, n % 2
-            for k in range(3):
+            for k in (2, 0, 1):
                 src_t = OQ[n][:, k, :, :] if k < 2 else OV[n][:]
                 nc.sync.dma_start(
                     out=outs[k][b, 0, 512 * ch : 512 * ch + 512, :].rearrange(
@@ -388,54 +404,65 @@ def tile_selectivetransformerlayer_pa_t_kernel(
                     in_=src_t.rearrange("p i d -> p (i d)"),
                 )
 
+        squares(0, ORDER8)
+        pairsum(0)
+        squares(1, ORDER8[0:4])
+        for tr in (trig_c, trig_s):
+            nc.scalar.activation(out=tr[:], in_=tr[:], func=ACT.Abs)
+            nc.scalar.activation(
+                out=tr[:], in_=tr[:], func=ACT.Sin, scale=-2.0 * math.pi, bias=half_pi[:, 0:1]
+            )
         pending = []
         cursor = [0]
-        for grp in range(2):
-            for op in fold_ops(grp):
-                fold_one(op)
-        for grp in range(2, 4):
-            pending.extend(fold_ops(grp))
+        for grp in range(len(GROUPS)):
+            if grp < VECTOR_GROUPS:
+                for op in fold_ops(grp):
+                    fold_one(nc.vector, op)
+            else:
+                pending.extend(fold_ops(grp))
 
         def ok(n):
             return 0 <= n < NCH
 
-        def body():
-            for k in range(-3, NCH):
-                if ok(k + 4) and k + 4 >= 2:
-                    load(k + 4)
-                if ok(k + 2):
-                    rstd(k + 2)
-                for hf in range(2):
-                    if ok(k + 1):
-                        evacuate(k + 1, hf)
-                        quantise(k + 1, hf)
-                    for i in (2 * hf, 2 * hf + 1):
-                        if ok(k):
-                            head_stats(k, i)
-                            rope_products(k, i)
-                        if ok(k + 3):
-                            squares(k + 3, i)
-                        if ok(k + 2):
-                            normalise(k + 2, i)
-                    if ok(k + 2):
-                        transposes(k + 2, hf)
-                    if ok(k + 1):
-                        project(k + 1, 2 * hf)
-                        project(k + 1, 2 * hf + 1)
-                    if ok(k):
-                        rope_add(k, hf)
-                    if k >= -1:
-                        for rep in range(2):
-                            if cursor[0] < len(pending):
-                                fold_one(pending[cursor[0]])
-                                cursor[0] = cursor[0] + 1
-                if ok(k + 3):
-                    pairsum(k + 3)
-                if ok(k):
-                    store(k)
-
-        if PINNED:
-            with tc.manual_schedule():
-                body()
-        else:
-            body()
+        for k in range(-3, NCH):
+            if ok(k + 6) and k + 6 >= 4:
+                load(k + 6)
+            if ok(k + 3):
+                rstd_root(k + 3)
+            if ok(k) and k < NCH - 1:
+                head_recip(k, 0, 4)
+                for i in range(4):
+                    rope_products(k, i)
+            if ok(k + 1):
+                evacuate(k + 1, 0)
+                evacuate(k + 1, 1)
+                quantise(k + 1)
+            if ok(k) and k < NCH - 1:
+                rope_add(nc.gpsimd, k, 0, 4)
+            if ok(k + 2):
+                transposes(k + 2, 0)
+                transposes(k + 2, 1)
+            if ok(k + 3):
+                rstd_recip(k + 3)
+                normalise(k + 3)
+            if ok(k + 4):
+                squares(k + 4, ORDER8[4:8] if k + 4 == 1 else ORDER8)
+            if ok(k + 1):
+                for i in range(4):
+                    project(k + 1, i)
+                    head_stats(k + 1, i)
+                    if k + 1 == NCH - 1:
+                        head_root(k + 1, i, 1)
+                        head_recip(k + 1, i, 1)
+                        rope_products(k + 1, i)
+                        rope_add(nc.vector if i % 2 else nc.gpsimd, k + 1, i, 1)
+                if k + 1 < NCH - 1:
+                    head_root(k + 1, 0, 4)
+            if ok(k + 4):
+                pairsum(k + 4)
+            if ok(k):
+                store(k)
+            for rep in range(FOLDS_PER_ROUND):
+                if cursor[0] < len(pending):
+                    fold_one(nc.gpsimd, pending[cursor[0]])
+                    cursor[0] = cursor[0] + 1

@@ -21,7 +21,7 @@ NCH = 16
 PINNED = True
 GROUPS = ((0, 4), (4, 4), (8, 8), (16, 8), (24, 8))
 VECTOR_GROUPS = 2
-FOLDS_PER_ROUND = 2
+NB = 6
 V_COPIES = ()
 ORDER8 = (0, 4, 1, 5, 2, 6, 3, 7)
 
@@ -41,9 +41,9 @@ def tile_selectivetransformerlayer_pa_t_kernel(
     outs = (out_0, out_1, out_2)
     with ExitStack() as ctx:
         const = ctx.enter_context(tc.tile_pool(name="const", bufs=1))
-        xpool = ctx.enter_context(tc.tile_pool(name="xpool", bufs=6))
+        xpool = ctx.enter_context(tc.tile_pool(name="xpool", bufs=8))
         hpool = ctx.enter_context(tc.tile_pool(name="hpool", bufs=3))
-        gpool = ctx.enter_context(tc.tile_pool(name="gpool", bufs=2))
+        gpool = ctx.enter_context(tc.tile_pool(name="gpool", bufs=3))
         ppool = ctx.enter_context(tc.tile_pool(name="ppool", bufs=2))
         opool = ctx.enter_context(tc.tile_pool(name="opool", bufs=3))
         small = ctx.enter_context(tc.tile_pool(name="small", bufs=8))
@@ -271,12 +271,13 @@ def tile_selectivetransformerlayer_pa_t_kernel(
             nc.vector.reciprocal(out=rs[:], in_=RT[n][:])
             RS[n] = rs
 
-        def normalise(n):
-            ht = hpool.tile([P, 8, 256], BF16, name="ht")
-            H[n] = ht
-            for g in ORDER8:
+        def normalise(n, gs):
+            if n not in H:
+                ht = hpool.tile([P, 8, 256], BF16, name="ht")
+                H[n] = ht
+            for g in gs:
                 nc.vector.scalar_tensor_tensor(
-                    out=ht[:, g, :],
+                    out=H[n][:, g, :],
                     in0=X[n][:, g, :],
                     scalar=RS[n][:, g : g + 1],
                     in1=spread[:, 0:256],
@@ -424,45 +425,57 @@ def tile_selectivetransformerlayer_pa_t_kernel(
         def ok(n):
             return 0 <= n < NCH
 
-        for k in range(-3, NCH):
-            if ok(k + 6) and k + 6 >= 4:
-                load(k + 6)
-            if ok(k + 3):
-                rstd_root(k + 3)
-            if ok(k) and k < NCH - 1:
-                head_recip(k, 0, 4)
+        squares(1, ORDER8[4:8])
+        for k in range(-5, NCH):
+            last = k == NCH - 1
+            if ok(k + 7) and k + 7 >= 4:
+                load(k + 7)
+            if ok(k + 4) and k + 4 >= 1:
+                pairsum(k + 4)
+            if ok(k) and not last:
                 for i in range(4):
-                    rope_products(k, i)
-            if ok(k + 1):
-                evacuate(k + 1, 0)
-                evacuate(k + 1, 1)
-                quantise(k + 1)
-            if ok(k) and k < NCH - 1:
-                rope_add(nc.gpsimd, k, 0, 4)
+                    head_stats(k, i)
+                head_root(k, 0, 4)
+            if ok(k + 4):
+                rstd_root(k + 4)
             if ok(k + 2):
                 transposes(k + 2, 0)
                 transposes(k + 2, 1)
             if ok(k + 3):
                 rstd_recip(k + 3)
-                normalise(k + 3)
-            if ok(k + 4):
-                squares(k + 4, ORDER8[4:8] if k + 4 == 1 else ORDER8)
+                normalise(k + 3, ORDER8[0:NB])
             if ok(k + 1):
+                quantise(k + 1)
+            if ok(k + 5) and k + 5 >= 2:
+                squares(k + 5, ORDER8[0:4])
+            if ok(k) and not last:
+                head_recip(k, 0, 4)
+                for i in range(4):
+                    rope_products(k, i)
+                    if ok(k + 1):
+                        project(k + 1, i)
+                    if i % 2 == 1:
+                        rope_add(nc.gpsimd, k, i - 1, 2)
+            elif last:
+                for i in range(4):
+                    head_stats(k, i)
+                    head_root(k, i, 1)
+                    head_recip(k, i, 1)
+                    rope_products(k, i)
+                    rope_add(nc.vector if i % 2 else nc.gpsimd, k, i, 1)
+            elif ok(k + 1):
                 for i in range(4):
                     project(k + 1, i)
-                    head_stats(k + 1, i)
-                    if k + 1 == NCH - 1:
-                        head_root(k + 1, i, 1)
-                        head_recip(k + 1, i, 1)
-                        rope_products(k + 1, i)
-                        rope_add(nc.vector if i % 2 else nc.gpsimd, k + 1, i, 1)
-                if k + 1 < NCH - 1:
-                    head_root(k + 1, 0, 4)
-            if ok(k + 4):
-                pairsum(k + 4)
+            if ok(k + 2):
+                evacuate(k + 2, 0)
+                evacuate(k + 2, 1)
+            if ok(k + 3):
+                normalise(k + 3, ORDER8[NB:8])
+            if ok(k + 5) and k + 5 >= 2:
+                squares(k + 5, ORDER8[4:8])
             if ok(k):
                 store(k)
-            for rep in range(FOLDS_PER_ROUND):
+            for rep in range(2 if (k < 0 or k in (0, 2, 4)) else 1):
                 if cursor[0] < len(pending):
                     fold_one(nc.gpsimd, pending[cursor[0]])
                     cursor[0] = cursor[0] + 1

@@ -22,6 +22,7 @@ PINNED = True
 GROUPS = ((0, 4), (4, 4), (8, 8), (16, 8), (24, 8))
 VECTOR_GROUPS = 2
 NB = 6
+FINE_FROM = 14
 V_COPIES = ()
 ORDER8 = (0, 4, 1, 5, 2, 6, 3, 7)
 
@@ -58,7 +59,6 @@ def tile_selectivetransformerlayer_pa_t_kernel(
 
         X = {}
         SS = {}
-        RT = {}
         RS = {}
         H = {}
         PT = {}
@@ -66,7 +66,6 @@ def tile_selectivetransformerlayer_pa_t_kernel(
         CD = {}
         PO = {}
         SQ = {}
-        R2 = {}
         RQ = {}
         PR = {}
         OQ = {}
@@ -76,13 +75,16 @@ def tile_selectivetransformerlayer_pa_t_kernel(
         def load(n):
             ch, b = n // 2, n % 2
             xt = xpool.tile([P, 8, 256], BF16, name="xt")
-            for j2 in range(2):
-                nc.sync.dma_start(
-                    out=xt[j2:P:2, :, :],
-                    in_=x[b, 512 * ch : 512 * ch + 512, 256 * j2 : 256 * j2 + 256].rearrange(
-                        "(a g) c -> a g c", g=8
-                    ),
-                )
+            pieces = 2 if n == 0 else 1
+            gp = 8 // pieces
+            for piece in range(pieces):
+                for j2 in range(2):
+                    nc.sync.dma_start(
+                        out=xt[j2:P:2, gp * piece : gp * piece + gp, :],
+                        in_=x[b, 512 * ch : 512 * ch + 512, 256 * j2 : 256 * j2 + 256].rearrange(
+                            "(a g) c -> a g c", g=8
+                        )[:, gp * piece : gp * piece + gp, :],
+                    )
             X[n] = xt
 
         for n in range(4):
@@ -136,9 +138,12 @@ def tile_selectivetransformerlayer_pa_t_kernel(
         )
         rate = const.tile([P, 44], F32, name="rate")
         for d, g in enumerate(turn_rates()):
-            nc.vector.tensor_scalar(
-                out=rate[:, d : d + 1], in0=ones[:], scalar1=g, scalar2=None, op0=ALU.mult
-            )
+            if d < 24:
+                nc.vector.tensor_scalar(
+                    out=rate[:, d : d + 1], in0=ones[:], scalar1=g, scalar2=None, op0=ALU.mult
+                )
+            else:
+                nc.scalar.activation(out=rate[:, d : d + 1], in_=ones[:], func=ACT.Copy, scale=g)
         pos_f = const.tile([P, 32], F32, name="pos_f")
         nc.vector.tensor_copy(out=pos_f[:], in_=pos_i[:])
 
@@ -260,15 +265,14 @@ def tile_selectivetransformerlayer_pa_t_kernel(
             SS[n] = pss
 
         def rstd_root(n):
-            root = small.tile([P, 8], F32, name="root")
-            nc.scalar.activation(
-                out=root[:], in_=SS[n][:], func=ACT.Sqrt, scale=1.0 / 512.0, bias=eps[:, 0:1]
-            )
-            RT[n] = root
-
-        def rstd_recip(n):
             rs = small.tile([P, 8], F32, name="rs")
-            nc.vector.reciprocal(out=rs[:], in_=RT[n][:])
+            nc.scalar.activation(
+                out=rs[:],
+                in_=SS[n][:],
+                func=ACT.Abs_reciprocal_sqrt,
+                scale=1.0 / 512.0,
+                bias=eps[:, 0:1],
+            )
             RS[n] = rs
 
         def normalise(n, gs):
@@ -349,19 +353,14 @@ def tile_selectivetransformerlayer_pa_t_kernel(
                 nc.scalar.copy(out=OV[n][:, i, :], in_=po[:, 384:512])
 
         def head_root(n, i0, ni):
-            root2 = small.tile([P, 4, 2], F32, name="root2")
+            rq = small.tile([P, 4, 2], F32, name="rq")
             nc.scalar.activation(
-                out=root2[:, i0 : i0 + ni, :],
+                out=rq[:, i0 : i0 + ni, :],
                 in_=SQ[n][:, i0 : i0 + ni, :],
-                func=ACT.Sqrt,
+                func=ACT.Abs_reciprocal_sqrt,
                 scale=1.0 / 128.0,
                 bias=eps[:, 0:1],
             )
-            R2[(n, i0)] = root2
-
-        def head_recip(n, i0, ni):
-            rq = small.tile([P, 4, 2], F32, name="rq")
-            nc.vector.reciprocal(out=rq[:, i0 : i0 + ni, :], in_=R2[(n, i0)][:, i0 : i0 + ni, :])
             for i in range(i0, i0 + ni):
                 RQ[(n, i)] = rq
 
@@ -405,7 +404,7 @@ def tile_selectivetransformerlayer_pa_t_kernel(
                     in_=src_t.rearrange("p i d -> p (i d)"),
                 )
 
-        squares(0, ORDER8)
+        squares(0, range(8))
         pairsum(0)
         squares(1, ORDER8[0:4])
         for tr in (trig_c, trig_s):
@@ -427,48 +426,44 @@ def tile_selectivetransformerlayer_pa_t_kernel(
 
         squares(1, ORDER8[4:8])
         for k in range(-5, NCH):
-            last = k == NCH - 1
+            fine = k >= FINE_FROM
             if ok(k + 7) and k + 7 >= 4:
                 load(k + 7)
-            if ok(k + 4) and k + 4 >= 1:
-                pairsum(k + 4)
-            if ok(k) and not last:
+            if ok(k) and not fine:
                 for i in range(4):
                     head_stats(k, i)
                 head_root(k, 0, 4)
-            if ok(k + 4):
-                rstd_root(k + 4)
             if ok(k + 2):
                 transposes(k + 2, 0)
                 transposes(k + 2, 1)
+            if ok(k + 4) and k + 4 >= 1:
+                pairsum(k + 4)
             if ok(k + 3):
-                rstd_recip(k + 3)
                 normalise(k + 3, ORDER8[0:NB])
             if ok(k + 1):
                 quantise(k + 1)
             if ok(k + 5) and k + 5 >= 2:
                 squares(k + 5, ORDER8[0:4])
-            if ok(k) and not last:
-                head_recip(k, 0, 4)
+            if ok(k):
                 for i in range(4):
+                    if fine:
+                        head_stats(k, i)
+                        head_root(k, i, 1)
                     rope_products(k, i)
                     if ok(k + 1):
                         project(k + 1, i)
-                    if i % 2 == 1:
+                    if k == NCH - 1:
+                        rope_add(nc.vector if i % 2 else nc.gpsimd, k, i, 1)
+                    elif i % 2 == 1:
                         rope_add(nc.gpsimd, k, i - 1, 2)
-            elif last:
-                for i in range(4):
-                    head_stats(k, i)
-                    head_root(k, i, 1)
-                    head_recip(k, i, 1)
-                    rope_products(k, i)
-                    rope_add(nc.vector if i % 2 else nc.gpsimd, k, i, 1)
             elif ok(k + 1):
                 for i in range(4):
                     project(k + 1, i)
             if ok(k + 2):
                 evacuate(k + 2, 0)
                 evacuate(k + 2, 1)
+            if ok(k + 4):
+                rstd_root(k + 4)
             if ok(k + 3):
                 normalise(k + 3, ORDER8[NB:8])
             if ok(k + 5) and k + 5 >= 2:

@@ -23,6 +23,7 @@ GROUPS = ((0, 4), (4, 4), (8, 8), (16, 8), (24, 8))
 VECTOR_GROUPS = 2
 NB = 6
 FINE_FROM = 14
+VECTOR_EVACUATES = 12
 V_COPIES = ()
 ORDER8 = (0, 4, 1, 5, 2, 6, 3, 7)
 
@@ -307,10 +308,16 @@ def tile_selectivetransformerlayer_pa_t_kernel(
             if hf == 0:
                 gq = gpool.tile([P, 2048], BF16, name="gq", align_bytes=64)
                 GQ[n] = gq
-            nc.scalar.copy(
-                out=GQ[n][:, 1024 * hf : 1024 * hf + 1024],
-                in_=PT[(n, hf)][:].rearrange("p i c -> p (i c)"),
-            )
+            if hf == 1 and n < VECTOR_EVACUATES:
+                nc.vector.tensor_copy(
+                    out=GQ[n][:, 1024 * hf : 1024 * hf + 1024],
+                    in_=PT[(n, hf)][:].rearrange("p i c -> p (i c)"),
+                )
+            else:
+                nc.scalar.copy(
+                    out=GQ[n][:, 1024 * hf : 1024 * hf + 1024],
+                    in_=PT[(n, hf)][:].rearrange("p i c -> p (i c)"),
+                )
 
         def quantise(n):
             codes = gpool.tile([P, 512], U32, name="codes", align_bytes=64)

@@ -23,7 +23,6 @@ GROUPS = ((0, 4), (4, 4), (8, 8), (16, 8), (24, 8))
 VECTOR_GROUPS = 2
 NB = 6
 FINE_FROM = 14
-VECTOR_EVACUATES = 12
 V_COPIES = ()
 ORDER8 = (0, 4, 1, 5, 2, 6, 3, 7)
 
@@ -308,16 +307,10 @@ def tile_selectivetransformerlayer_pa_t_kernel(
             if hf == 0:
                 gq = gpool.tile([P, 2048], BF16, name="gq", align_bytes=64)
                 GQ[n] = gq
-            if hf == 1 and n < VECTOR_EVACUATES:
-                nc.vector.tensor_copy(
-                    out=GQ[n][:, 1024 * hf : 1024 * hf + 1024],
-                    in_=PT[(n, hf)][:].rearrange("p i c -> p (i c)"),
-                )
-            else:
-                nc.scalar.copy(
-                    out=GQ[n][:, 1024 * hf : 1024 * hf + 1024],
-                    in_=PT[(n, hf)][:].rearrange("p i c -> p (i c)"),
-                )
+            nc.scalar.copy(
+                out=GQ[n][:, 1024 * hf : 1024 * hf + 1024],
+                in_=PT[(n, hf)][:].rearrange("p i c -> p (i c)"),
+            )
 
         def quantise(n):
             codes = gpool.tile([P, 512], U32, name="codes", align_bytes=64)
@@ -431,6 +424,12 @@ def tile_selectivetransformerlayer_pa_t_kernel(
         def ok(n):
             return 0 <= n < NCH
 
+        def folds(k):
+            for rep in range(2 if (k < 0 or k in (0, 2, 4)) else 1):
+                if cursor[0] < len(pending):
+                    fold_one(nc.gpsimd, pending[cursor[0]])
+                    cursor[0] = cursor[0] + 1
+
         squares(1, ORDER8[4:8])
         for k in range(-5, NCH):
             fine = k >= FINE_FROM
@@ -461,11 +460,17 @@ def tile_selectivetransformerlayer_pa_t_kernel(
                         project(k + 1, i)
                     if k == NCH - 1:
                         rope_add(nc.vector if i % 2 else nc.gpsimd, k, i, 1)
-                    elif i % 2 == 1:
-                        rope_add(nc.gpsimd, k, i - 1, 2)
-            elif ok(k + 1):
-                for i in range(4):
-                    project(k + 1, i)
+                    elif i < 2:
+                        rope_add(nc.gpsimd, k, i, 1)
+                    elif i == 3:
+                        rope_add(nc.gpsimd, k, 2, 2)
+                    if i == 0:
+                        folds(k)
+            else:
+                if ok(k + 1):
+                    for i in range(4):
+                        project(k + 1, i)
+                folds(k)
             if ok(k + 2):
                 evacuate(k + 2, 0)
                 evacuate(k + 2, 1)
@@ -477,7 +482,3 @@ def tile_selectivetransformerlayer_pa_t_kernel(
                 squares(k + 5, ORDER8[4:8])
             if ok(k):
                 store(k)
-            for rep in range(2 if (k < 0 or k in (0, 2, 4)) else 1):
-                if cursor[0] < len(pending):
-                    fold_one(nc.gpsimd, pending[cursor[0]])
-                    cursor[0] = cursor[0] + 1

import math
from contextlib import ExitStack

import concourse.mybir as mybir
from concourse.masks import make_identity

F32 = mybir.dt.float32
BF16 = mybir.dt.bfloat16
I32 = mybir.dt.int32
U32 = mybir.dt.uint32
U8 = mybir.dt.uint8
FP8X4 = mybir.dt.float8_e4m3fn_x4
ACT = mybir.ActivationFunctionType
ALU = mybir.AluOpType

P = 128
FLOPS = 2 * 8192 * 512 * 384
ROPE_BASE = 1000000.0
EPS = 1e-6
NCH = 16
PINNED = True
GROUPS = ((0, 4), (4, 4), (8, 8), (16, 8), (24, 8))
VECTOR_GROUPS = 2
NB = 6
FINE_FROM = 14
V_COPIES = ()
ORDER8 = (0, 4, 1, 5, 2, 6, 3, 7)


def turn_rates():
    rates = []
    for sd in (48, 40):
        for j in range(sd // 2):
            rates.append(1.0 / ROPE_BASE ** (2.0 * j / sd) / (2.0 * math.pi))
    return rates


def tile_selectivetransformerlayer_pa_t_kernel(
    tc, x, ln1_w, wq, wk, wv, q_norm_w, k_norm_w, out_0, out_1, out_2
):
    nc = tc.nc
    outs = (out_0, out_1, out_2)
    with ExitStack() as ctx:
        const = ctx.enter_context(tc.tile_pool(name="const", bufs=1))
        xpool = ctx.enter_context(tc.tile_pool(name="xpool", bufs=8))
        hpool = ctx.enter_context(tc.tile_pool(name="hpool", bufs=3))
        gpool = ctx.enter_context(tc.tile_pool(name="gpool", bufs=3))
        ppool = ctx.enter_context(tc.tile_pool(name="ppool", bufs=2))
        opool = ctx.enter_context(tc.tile_pool(name="opool", bufs=3))
        small = ctx.enter_context(tc.tile_pool(name="small", bufs=8))
        junkp = ctx.enter_context(tc.tile_pool(name="junkp", bufs=4))
        ps_w = ctx.enter_context(tc.psum_pool(name="ps_w", bufs=1))
        ps_s = ctx.enter_context(tc.psum_pool(name="ps_s", bufs=1))
        ps_t = ctx.enter_context(tc.psum_pool(name="ps_t", bufs=2))
        ps_o = ctx.enter_context(tc.psum_pool(name="ps_o", bufs=4))

        if PINNED:
            ctx.enter_context(tc.manual_schedule())

        X = {}
        SS = {}
        RS = {}
        H = {}
        PT = {}
        GQ = {}
        CD = {}
        PO = {}
        SQ = {}
        RQ = {}
        PR = {}
        OQ = {}
        OV = {}
        TAB = {}

        def load(n):
            ch, b = n // 2, n % 2
            xt = xpool.tile([P, 8, 256], BF16, name="xt")
            pieces = 2 if n == 0 else 1
            gp = 8 // pieces
            for piece in range(pieces):
                for j2 in range(2):
                    nc.sync.dma_start(
                        out=xt[j2:P:2, gp * piece : gp * piece + gp, :],
                        in_=x[b, 512 * ch : 512 * ch + 512, 256 * j2 : 256 * j2 + 256].rearrange(
                            "(a g) c -> a g c", g=8
                        )[:, gp * piece : gp * piece + gp, :],
                    )
            X[n] = xt

        for n in range(4):
            load(n)

        ones = const.tile([P, 1], F32, name="ones")
        nc.vector.memset(ones[:], 1.0)
        sel = const.tile([P, 64, 2], BF16, name="sel")
        nc.vector.memset(sel[:], 0.0)
        nc.vector.memset(sel[0:1, :, 0], 1.0)
        nc.vector.memset(sel[32:33, :, 1], 1.0)
        rows = const.tile([P, 512], BF16, name="rows")
        nc.vector.memset(rows[:], 0.0)
        for r, half in ((0, 0), (32, 1)):
            nc.scalar.dma_start(
                out=rows[r : r + 1, 0:256],
                in_=ln1_w[256 * half : 256 * half + 256].rearrange("(o n) -> o n", o=1),
            )
        w_sb = const.tile([P, 3, 512], BF16, name="w_sb")
        for wi, w in enumerate((wq, wk, wv)):
            nc.scalar.dma_start(out=w_sb[:, wi, :], in_=w)
        for r in (0, 32):
            nc.scalar.dma_start(
                out=rows[r : r + 1, 256:384], in_=q_norm_w.rearrange("(o n) -> o n", o=1)
            )
            nc.scalar.dma_start(
                out=rows[r : r + 1, 384:512], in_=k_norm_w.rearrange("(o n) -> o n", o=1)
            )
        warm = const.tile([P, 1], F32, name="warm")
        nc.scalar.activation(out=warm[:], in_=ones[:], func=ACT.Sin)

        ident_f = const.tile([P, P], F32, name="ident_f")
        make_identity(nc, ident_f[:])
        pos_i = const.tile([P, 32], I32, name="pos_i")
        nc.gpsimd.iota(pos_i[:], pattern=[[512, 8], [1, 4]], base=0, channel_multiplier=4)

        ident_b = const.tile([P, P], BF16, name="ident_b")
        nc.vector.tensor_copy(out=ident_b[:], in_=ident_f[:])
        idv = ident_f[:].rearrange("p (a e) -> p a e", e=2)
        pair_half = const.tile([P, 64], F32, name="pair_half")
        nc.vector.tensor_tensor(out=pair_half[:], in0=idv[:, :, 0], in1=idv[:, :, 1], op=ALU.add)
        pair_sum = const.tile([P, 64, 2], F32, name="pair_sum")
        nc.vector.tensor_copy(
            out=pair_sum[:], in_=pair_half[:].unsqueeze(2).to_broadcast([P, 64, 2])
        )
        eps = const.tile([P, 1], F32, name="eps")
        nc.vector.tensor_scalar(out=eps[:], in0=ones[:], scalar1=EPS, scalar2=None, op0=ALU.mult)
        half_pi = const.tile([P, 1], F32, name="half_pi")
        nc.vector.tensor_scalar(
            out=half_pi[:], in0=ones[:], scalar1=math.pi / 2.0, scalar2=None, op0=ALU.mult
        )
        rate = const.tile([P, 44], F32, name="rate")
        for d, g in enumerate(turn_rates()):
            if d < 24:
                nc.vector.tensor_scalar(
                    out=rate[:, d : d + 1], in0=ones[:], scalar1=g, scalar2=None, op0=ALU.mult
                )
            else:
                nc.scalar.activation(out=rate[:, d : d + 1], in_=ones[:], func=ACT.Copy, scale=g)
        pos_f = const.tile([P, 32], F32, name="pos_f")
        nc.vector.tensor_copy(out=pos_f[:], in_=pos_i[:])

        spread = ps_w.tile([P, 512], F32, name="spread")
        nc.tensor.matmul(
            out=spread[:],
            lhsT=sel[:].rearrange("p a e -> p (a e)"),
            rhs=rows[:],
            start=True,
            stop=True,
        )

        turns = const.tile([P, 32, 44], F32, name="turns")
        nc.vector.tensor_tensor(
            out=turns[:],
            in0=pos_f[:].unsqueeze(2).to_broadcast([P, 32, 44]),
            in1=rate[:].unsqueeze(1).to_broadcast([P, 32, 44]),
            op=ALU.mult,
        )
        whole_c = const.tile([P, 32, 44], I32, name="whole_c")
        nc.vector.tensor_copy(out=whole_c[:], in_=turns[:])
        trig_c = const.tile([P, 32, 44], F32, name="trig_c")
        nc.vector.tensor_tensor(out=trig_c[:], in0=turns[:], in1=whole_c[:], op=ALU.subtract)
        whole_s = const.tile([P, 32, 44], I32, name="whole_s")
        nc.vector.tensor_scalar(
            out=whole_s[:], in0=turns[:], scalar1=-0.25, scalar2=None, op0=ALU.add
        )
        trig_s = const.tile([P, 32, 44], F32, name="trig_s")
        nc.vector.scalar_tensor_tensor(
            out=trig_s[:],
            in0=turns[:],
            scalar=-0.25,
            in1=whole_s[:],
            op0=ALU.add,
            op1=ALU.subtract,
        )

        gw = const.tile([P, 512, 4], BF16, name="gw", align_bytes=64)
        for wi in range(3):
            pw = ps_t.tile([P, 2, 512], BF16, name="pt")
            for t in range(4):
                blk = 2 * (t % 2) + t // 2
                nc.tensor.transpose(
                    out=pw[:, 0, 128 * t : 128 * t + 128],
                    in_=w_sb[:, wi, 128 * blk : 128 * blk + 128],
                    identity=ident_b[:],
                )
            src = pw[:, 0, :].rearrange("p (t n) -> p n t", t=4)
            base = 192 * wi
            nc.vector.tensor_copy(out=gw[:, base : base + 128, :], in_=src)
            if wi < 2:
                nc.vector.tensor_copy(out=gw[:, base + 128 : base + 192, :], in_=src[:, 0:64, :])
        w_codes = const.tile([P, 512], U32, name="w_codes", align_bytes=64)
        w_scales = const.tile([P, 512], U8, name="w_scales", align_bytes=64)
        nc.vector.quantize_mx(
            out=w_codes[:].bitcast(FP8X4),
            scales=w_scales[:],
            in_=gw[:].rearrange("p n t -> p (n t)"),
        )

        wn = spread[:, 256:512].rearrange("p (q h c) -> p q h c", q=2, h=2)
        w_cos = const.tile([P, 2, 2, 64], F32, name="w_cos")
        nc.vector.tensor_copy(out=w_cos[:], in_=wn)
        w_sin = const.tile([P, 2, 2, 64], F32, name="w_sin")
        nc.vector.tensor_scalar(
            out=w_sin[:, :, 0, :], in0=wn[:, :, 1, :], scalar1=-1.0, scalar2=None, op0=ALU.mult
        )
        nc.vector.tensor_copy(out=w_sin[:, :, 1, :], in_=wn[:, :, 0, :])

        def fold_ops(grp):
            t0, nt = GROUPS[grp]
            tab = const.tile([P, 2, nt, 2, 128], F32, name="tab%d" % grp)
            TAB[grp] = tab
            ops = []
            for ab, (tr, wrow) in enumerate(((trig_c, w_cos), (trig_s, w_sin))):
                wflat = wrow[:].rearrange("p q h c -> p q (h c)")
                for qk in range(2):
                    for c0, reps, d0, nd in ((0, 2, 0, 24), (48, 4, 24, 20)):
                        ops.append((tab, ab, qk, c0, reps, d0, nd, tr, wflat, t0, nt))
            return ops

        def fold_one(eng, op):
            tab, ab, qk, c0, reps, d0, nd, tr, wflat, t0, nt = op
            eng.tensor_tensor(
                out=tab[:, ab, :, qk, c0 : c0 + reps * nd].rearrange("p t (r d) -> p t r d", r=reps),
                in0=tr[:, t0 : t0 + nt, d0 : d0 + nd].unsqueeze(2).to_broadcast([P, nt, reps, nd]),
                in1=wflat[:, qk, c0 : c0 + reps * nd]
                .rearrange("p (r d) -> p r d", r=reps)
                .unsqueeze(1)
                .to_broadcast([P, nt, reps, nd]),
                op=ALU.mult,
            )

        def table_of(tau):
            for grp, (t0, nt) in enumerate(GROUPS):
                if t0 <= tau < t0 + nt:
                    return TAB[grp], tau - t0
            return None, 0

        def squares(n, gs):
            if n not in SS:
                ss = small.tile([P, 8], F32, name="ss")
                SS[n] = ss
            for g in gs:
                junk = junkp.tile([P, 256], BF16, name="junk")
                nc.scalar.activation(
                    out=junk[:], in_=X[n][:, g, :], func=ACT.Square, accum_out=SS[n][:, g : g + 1]
                )

        def pairsum(n):
            pss = ps_s.tile([P, 8], F32, name="pss")
            nc.tensor.matmul(
                out=pss[:],
                lhsT=pair_sum[:].rearrange("p a e -> p (a e)"),
                rhs=SS[n][:],
                start=True,
                stop=True,
            )
            SS[n] = pss

        def rstd_root(n):
            rs = small.tile([P, 8], F32, name="rs")
            nc.scalar.activation(
                out=rs[:],
                in_=SS[n][:],
                func=ACT.Abs_reciprocal_sqrt,
                scale=1.0 / 512.0,
                bias=eps[:, 0:1],
            )
            RS[n] = rs

        def normalise(n, gs):
            if n not in H:
                ht = hpool.tile([P, 8, 256], BF16, name="ht")
                H[n] = ht
            for g in gs:
                nc.vector.scalar_tensor_tensor(
                    out=H[n][:, g, :],
                    in0=X[n][:, g, :],
                    scalar=RS[n][:, g : g + 1],
                    in1=spread[:, 0:256],
                    op0=ALU.mult,
                    op1=ALU.mult,
                )

        def transposes(n, hf):
            pt = ps_t.tile([P, 2, 512], BF16, name="pt")
            PT[(n, hf)] = pt
            for i2 in range(2):
                i = 2 * hf + i2
                view = pt[:, i2, :].rearrange("p (a r e) -> p a r e", r=4, e=2)
                for hh in range(2):
                    for u in range(2):
                        nc.tensor.transpose(
                            out=view[:, :, 2 * hh + u, :],
                            in_=H[n][:, 4 * hh + i, 128 * u : 128 * u + 128],
                            identity=ident_b[:],
                        )

        def evacuate(n, hf):
            if hf == 0:
                gq = gpool.tile([P, 2048], BF16, name="gq", align_bytes=64)
                GQ[n] = gq
            nc.scalar.copy(
                out=GQ[n][:, 1024 * hf : 1024 * hf + 1024],
                in_=PT[(n, hf)][:].rearrange("p i c -> p (i c)"),
            )

        def quantise(n):
            codes = gpool.tile([P, 512], U32, name="codes", align_bytes=64)
            scl = gpool.tile([P, 512], U8, name="scl", align_bytes=64)
            CD[n] = (codes, scl)
            nc.vector.quantize_mx(out=codes[:].bitcast(FP8X4), scales=scl[:], in_=GQ[n][:])

        def project(n, i):
            codes, scl = CD[n]
            po = ps_o.tile([P, 512], F32, name="po")
            PO[(n, i)] = po
            nc.tensor.matmul_mx(
                out=po[:],
                lhsT=codes[:, 128 * i : 128 * i + 128].bitcast(FP8X4),
                lhsT_scale=scl[:, 128 * i : 128 * i + 128],
                rhs=w_codes[:].bitcast(FP8X4),
                rhs_scale=w_scales[:],
                start=True,
                stop=True,
            )

        def head_stats(n, i):
            po = PO[(n, i)]
            if i == 0:
                ov = opool.tile([P, 4, 128], F32, name="ov")
                OV[n] = ov
                sq = small.tile([P, 4, 2], F32, name="sq")
                SQ[n] = sq
            for qk in range(2):
                junk2 = junkp.tile([P, 128], BF16, name="junk2")
                nc.scalar.activation(
                    out=junk2[:],
                    in_=po[:, 192 * qk : 192 * qk + 128],
                    func=ACT.Square,
                    accum_out=SQ[n][:, i, qk : qk + 1],
                )
            if i in V_COPIES:
                nc.vector.tensor_copy(out=OV[n][:, i, :], in_=po[:, 384:512])
            else:
                nc.scalar.copy(out=OV[n][:, i, :], in_=po[:, 384:512])

        def head_root(n, i0, ni):
            rq = small.tile([P, 4, 2], F32, name="rq")
            nc.scalar.activation(
                out=rq[:, i0 : i0 + ni, :],
                in_=SQ[n][:, i0 : i0 + ni, :],
                func=ACT.Abs_reciprocal_sqrt,
                scale=1.0 / 128.0,
                bias=eps[:, 0:1],
            )
            for i in range(i0, i0 + ni):
                RQ[(n, i)] = rq

        def rope_products(n, i):
            po = PO[(n, i)]
            rq = RQ[(n, i)]
            if i == 0:
                pr = ppool.tile([P, 2, 4, 2, 128], F32, name="pr")
                PR[n] = pr
            tab, tl = table_of(4 * (n // 2) + i)
            for qk in range(2):
                for ab in range(2):
                    nc.vector.scalar_tensor_tensor(
                        out=PR[n][:, qk, i, ab, :],
                        in0=po[:, 192 * qk + 64 * ab : 192 * qk + 64 * ab + 128],
                        scalar=rq[:, i, qk : qk + 1],
                        in1=tab[:, ab, tl, qk, :],
                        op0=ALU.mult,
                        op1=ALU.mult,
                    )

        def rope_add(eng, n, i0, ni):
            if i0 == 0:
                oq = opool.tile([P, 2, 4, 128], F32, name="oq")
                OQ[n] = oq
            eng.tensor_tensor(
                out=OQ[n][:, :, i0 : i0 + ni, :],
                in0=PR[n][:, :, i0 : i0 + ni, 0, :],
                in1=PR[n][:, :, i0 : i0 + ni, 1, :],
                op=ALU.add,
            )

        def store(n):
            ch, b = n // 2, n % 2
            for k in (2, 0, 1):
                src_t = OQ[n][:, k, :, :] if k < 2 else OV[n][:]
                nc.sync.dma_start(
                    out=outs[k][b, 0, 512 * ch : 512 * ch + 512, :].rearrange(
                        "(m i) d -> m (i d)", i=4
                    ),
                    in_=src_t.rearrange("p i d -> p (i d)"),
                )

        squares(0, range(8))
        pairsum(0)
        squares(1, ORDER8[0:4])
        for tr in (trig_c, trig_s):
            nc.scalar.activation(out=tr[:], in_=tr[:], func=ACT.Abs)
            nc.scalar.activation(
                out=tr[:], in_=tr[:], func=ACT.Sin, scale=-2.0 * math.pi, bias=half_pi[:, 0:1]
            )
        pending = []
        cursor = [0]
        for grp in range(len(GROUPS)):
            if grp < VECTOR_GROUPS:
                for op in fold_ops(grp):
                    fold_one(nc.vector, op)
            else:
                pending.extend(fold_ops(grp))

        def ok(n):
            return 0 <= n < NCH

        def folds(k):
            for rep in range(2 if (k < 0 or k in (0, 2, 4)) else 1):
                if cursor[0] < len(pending):
                    fold_one(nc.gpsimd, pending[cursor[0]])
                    cursor[0] = cursor[0] + 1

        squares(1, ORDER8[4:8])
        for k in range(-5, NCH):
            fine = k >= FINE_FROM
            if ok(k + 7) and k + 7 >= 4:
                load(k + 7)
            if ok(k) and not fine:
                for i in range(4):
                    head_stats(k, i)
                head_root(k, 0, 4)
            if ok(k + 2):
                transposes(k + 2, 0)
                transposes(k + 2, 1)
            if ok(k + 4) and k + 4 >= 1:
                pairsum(k + 4)
            if ok(k + 3):
                normalise(k + 3, ORDER8[0:NB])
            if ok(k + 1):
                quantise(k + 1)
            if ok(k + 5) and k + 5 >= 2:
                squares(k + 5, ORDER8[0:4])
            if ok(k):
                for i in range(4):
                    if fine:
                        head_stats(k, i)
                        head_root(k, i, 1)
                    rope_products(k, i)
                    if ok(k + 1):
                        project(k + 1, i)
                    if k == NCH - 1:
                        rope_add(nc.vector if i % 2 else nc.gpsimd, k, i, 1)
                    elif i < 2:
                        rope_add(nc.gpsimd, k, i, 1)
                    elif i == 3:
                        rope_add(nc.gpsimd, k, 2, 2)
                    if i == 0:
                        folds(k)
            else:
                if ok(k + 1):
                    for i in range(4):
                        project(k + 1, i)
                folds(k)
            if ok(k + 2):
                evacuate(k + 2, 0)
                evacuate(k + 2, 1)
            if ok(k + 4):
                rstd_root(k + 4)
            if ok(k + 3):
                normalise(k + 3, ORDER8[NB:8])
            if ok(k + 5) and k + 5 >= 2:
                squares(k + 5, ORDER8[4:8])
            if ok(k):
                store(k)
